import numpy as np
import ml_dtypes


def mxq(x, axis, fmt="e4m3"):
    dtype, down = {"e4m3": (ml_dtypes.float8_e4m3fn, 7), "e5m2": (ml_dtypes.float8_e5m2, 14)}[fmt]
    v = np.moveaxis(np.asarray(x, np.float32).astype(ml_dtypes.bfloat16).astype(np.float64), axis, -1)
    blocks = v.reshape(v.shape[:-1] + (-1, 32))
    amax = np.abs(blocks).max(-1, keepdims=True)
    byte = np.maximum(np.where(amax > 0, np.frexp(amax)[1] - 1 + 127, 0) - down, 1)
    scale = np.exp2(byte - 127.0)
    codes = (blocks / scale).astype(np.float32).astype(dtype).astype(np.float64)
    return np.moveaxis((codes * scale).reshape(v.shape), -1, axis)


WIDE = False


def mx_kscale(k):
    if not WIDE:
        return np.ones(k)
    levels = np.array([20, -20, 10, -10, 0])
    a = np.random.permutation(np.resize(levels, k // 512 * 4)).reshape(k // 512, 4)
    idx = np.arange(k)
    return np.exp2(a[idx // 512, idx % 128 // 32])


BF16 = ml_dtypes.bfloat16


def bf(x):
    return np.asarray(x, np.float32).astype(BF16)


def f64(x):
    return np.asarray(x).astype(np.float64)


B, S, I0, I1, I2, O0, O1, O2 = 2, 256, 1024, 2048, 4096, 1024, 1024, 2048
O = O0 + O1 + O2
GS = 8.0


def init_w(out_d, in_d, u):
    return bf(np.random.uniform(-1.0, 1.0, (out_d, in_d)) / np.sqrt(in_d) / u[:, None])


def setup_inputs():
    u = mx_kscale(O)
    x = bf(np.random.standard_normal((B, S, I2)))
    W0 = init_w(O0, I0, u[:O0])
    W1 = init_w(O1, I1, u[O0:O0 + O1])
    W2 = init_w(O2, I2, u[O0 + O1:])
    g = np.random.standard_normal((B, S, O)) * np.exp2(np.random.randint(-12, 1, (B, S, 1))) * GS * u
    return {"x": x, "W0": W0, "W1": W1, "W2": W2, "grad_out": bf(g)}


def reference(x, W0, W1, W2, grad_out):
    gq = mxq(f64(grad_out), 2, "e5m2")
    p0 = gq[..., :O0] @ mxq(f64(W0), 0, "e4m3")
    p1 = gq[..., O0:O0 + O1] @ mxq(f64(W1), 0, "e4m3")
    p2 = gq[..., O0 + O1:] @ mxq(f64(W2), 0, "e4m3")
    out = np.array(p2, dtype=np.float64)
    out[..., :I1] = out[..., :I1] + p1
    out[..., :I0] = out[..., :I0] + p0
    return out

@@ -1,0 +1,157 @@
+from contextlib import ExitStack
+
+import concourse.mybir as mybir
+from concourse.masks import make_identity
+
+F32 = mybir.dt.float32
+BF16 = mybir.dt.bfloat16
+U32 = mybir.dt.uint32
+U8 = mybir.dt.uint8
+E4X4 = mybir.dt.float8_e4m3fn_x4
+E5X4 = mybir.dt.float8_e5m2_x4
+
+P = 128
+TOKENS = 512
+FEATURES = 4096
+TOK_TILES = TOKENS // P
+K_PASS = 512
+N_PASS = FEATURES // K_PASS
+BLOCK = 512
+RANGE = 1024
+N_RANGES = FEATURES // RANGE
+
+FLOPS = 2 * TOKENS * (1024 * 1024 + 1024 * 2048 + 2048 * 4096)
+BYTES = 2 * (1024 * 1024 + 1024 * 2048 + 2048 * 4096) + 2 * TOKENS * FEATURES + 4 * TOKENS * FEATURES
+
+
+def first_pass_of_range(r):
+    if r == 0:
+        return 0
+    if r == 1:
+        return 2
+    return 4
+
+
+def tile_naivematryoshkalinear_kernel(tc, x, W0, W1, W2, grad_out, out):
+    nc = tc.nc
+    g = grad_out.flatten_outer_dims()
+    o = out.flatten_outer_dims()
+
+    def weight_rows(c):
+        if c < 2:
+            return W0, K_PASS * c
+        if c < 4:
+            return W1, K_PASS * (c - 2)
+        return W2, K_PASS * (c - 4)
+
+    with ExitStack() as ctx:
+        const = ctx.enter_context(tc.tile_pool(name="const", bufs=1))
+        graw_pool = ctx.enter_context(tc.tile_pool(name="graw", bufs=4))
+        ggrp_pool = ctx.enter_context(tc.tile_pool(name="ggrp", bufs=2))
+        raw_pool = ctx.enter_context(tc.tile_pool(name="raw", bufs=8))
+        grp_pool = ctx.enter_context(tc.tile_pool(name="grp", bufs=3))
+        code_pool = ctx.enter_context(tc.tile_pool(name="code", bufs=8))
+        ost_pool = ctx.enter_context(tc.tile_pool(name="ost", bufs=6))
+        psum = ctx.enter_context(tc.psum_pool(name="psum", bufs=8))
+
+        ident = const.tile([P, P], F32, name="ident")
+        make_identity(nc, ident[:])
+        g_codes = const.tile([P, TOK_TILES, N_PASS * P], U32, name="g_codes", align_bytes=64)
+        g_scales = const.tile([P, TOK_TILES, N_PASS * P], U8, name="g_scales", align_bytes=64)
+
+        g_raw = []
+        for t in range(TOK_TILES):
+            gr = graw_pool.tile([P, FEATURES], BF16, name="g_raw", tag="g_raw")
+            nc.sync.dma_start(out=gr[:], in_=g[P * t : P * t + P, :])
+            g_raw.append(gr)
+
+        for t in range(TOK_TILES):
+            words = g_raw[t][:].bitcast(F32)
+            g_grp = ggrp_pool.tile([P, FEATURES], BF16, name="g_grp", tag="g_grp", align_bytes=64)
+            grp_words = g_grp[:].bitcast(F32)
+            for b in range(4):
+                xt = psum.tile([P, 4, P], F32, name="xt", tag="bank")
+                for q in range(4):
+                    w0 = 512 * b + P * q
+                    nc.tensor.transpose(xt[:, q, :], words[:, w0 : w0 + P], ident[:])
+                dst = grp_words[:, 512 * b : 512 * b + 512].rearrange("p (c r u) -> p c r u", c=2, u=2)
+                src = xt[:].rearrange("p (c u) r -> p c r u", u=2)
+                if b % 2 == 0:
+                    nc.vector.tensor_copy(out=dst, in_=src)
+                else:
+                    nc.scalar.copy(out=dst, in_=src)
+            nc.vector.quantize_mx(
+                out=g_codes[:, t, :].bitcast(E5X4), scales=g_scales[:, t, :], in_=g_grp[:]
+            )
+
+        chunks = [(r, c) for r in range(N_RANGES) for c in range(first_pass_of_range(r), N_PASS)]
+        n = len(chunks)
+        raws = {}
+        grps = {}
+        codes = {}
+        accs = {}
+
+        def load(s):
+            r, c = chunks[s]
+            w, row0 = weight_rows(c)
+            raw = raw_pool.tile([P, 4, RANGE], BF16, name="raw", tag="raw")
+            for u in range(2):
+                rows = w[row0 + 256 * u : row0 + 256 * u + 256, RANGE * r : RANGE * r + RANGE]
+                nc.sync.dma_start(out=raw[:, 2 * u : 2 * u + 2, :], in_=rows.rearrange("(p e) w -> p e w", e=2))
+            raws[s] = raw
+
+        def regroup(s):
+            raw = raws[s]
+            for j in range(2):
+                tag = "grp_v" if j == 0 else "grp_s"
+                grp = grp_pool.tile([P, BLOCK, 4], BF16, name=tag, tag=tag, align_bytes=64)
+                dst = grp[:].rearrange("p (c i) t -> p c t i", i=4)
+                src = raw[:, :, BLOCK * j : BLOCK * j + BLOCK].rearrange("p t (c i) -> p c t i", i=4)
+                if j == 0:
+                    nc.vector.tensor_copy(out=dst, in_=src)
+                else:
+                    nc.scalar.copy(out=dst, in_=src)
+                grps[(s, j)] = grp
+
+        def quantise(s):
+            for j in range(2):
+                cw = code_pool.tile([P, BLOCK], U32, name="w_codes", tag="w_codes", align_bytes=64)
+                cs = code_pool.tile([P, BLOCK], U8, name="w_scales", tag="w_scales", align_bytes=64)
+                nc.vector.quantize_mx(
+                    out=cw[:].bitcast(E4X4), scales=cs[:], in_=grps[(s, j)][:].rearrange("p w t -> p (w t)")
+                )
+                codes[(s, j)] = (cw, cs)
+
+        def multiply(s):
+            r, c = chunks[s]
+            first = c == first_pass_of_range(r)
+            last = c == N_PASS - 1
+            for t in range(TOK_TILES):
+                for j in range(2):
+                    if first:
+                        accs[(t, j)] = psum.tile([P, BLOCK], F32, name="acc", tag="bank")
+                    cw, cs = codes[(s, j)]
+                    nc.tensor.matmul_mx(
+                        out=accs[(t, j)][:],
+                        lhsT=g_codes[:, t, P * c : P * c + P].bitcast(E5X4),
+                        lhsT_scale=g_scales[:, t, P * c : P * c + P],
+                        rhs=cw[:].bitcast(E4X4),
+                        rhs_scale=cs[:],
+                        start=first,
+                        stop=last,
+                    )
+            if last:
+                for t in range(TOK_TILES):
+                    ost = ost_pool.tile([P, RANGE], F32, name="ost", tag="ost")
+                    nc.vector.tensor_copy(out=ost[:, 0:BLOCK], in_=accs[(t, 0)][:])
+                    nc.scalar.copy(out=ost[:, BLOCK:RANGE], in_=accs[(t, 1)][:])
+                    nc.sync.dma_start(out=o[P * t : P * t + P, RANGE * r : RANGE * r + RANGE], in_=ost[:])
+
+        for s in range(n + 2):
+            if s < n:
+                load(s)
+                regroup(s)
+            if 1 <= s <= n:
+                quantise(s - 1)
+            if s >= 2:
+                multiply(s - 2)

@@ -19,6 +19,11 @@ N_PASS = FEATURES // K_PASS
 BLOCK = 512
 RANGE = 1024
 N_RANGES = FEATURES // RANGE
+VCOLS = 608
+RAW_BUFS = 8
+EVAC = "SSSSSSSS"
+EVAC_LAST = "VSVSVSVS"
+GCOPY = "VSVS"
 
 FLOPS = 2 * TOKENS * (1024 * 1024 + 1024 * 2048 + 2048 * 4096)
 BYTES = 2 * (1024 * 1024 + 1024 * 2048 + 2048 * 4096) + 2 * TOKENS * FEATURES + 4 * TOKENS * FEATURES
@@ -48,22 +53,47 @@ def tile_naivematryoshkalinear_kernel(tc, x, W0, W1, W2, grad_out, out):
         const = ctx.enter_context(tc.tile_pool(name="const", bufs=1))
         graw_pool = ctx.enter_context(tc.tile_pool(name="graw", bufs=4))
         ggrp_pool = ctx.enter_context(tc.tile_pool(name="ggrp", bufs=2))
-        raw_pool = ctx.enter_context(tc.tile_pool(name="raw", bufs=8))
-        grp_pool = ctx.enter_context(tc.tile_pool(name="grp", bufs=3))
-        code_pool = ctx.enter_context(tc.tile_pool(name="code", bufs=8))
-        ost_pool = ctx.enter_context(tc.tile_pool(name="ost", bufs=6))
+        raw_pool = ctx.enter_context(tc.tile_pool(name="raw", bufs=RAW_BUFS))
+        grp_pool = ctx.enter_context(tc.tile_pool(name="grp", bufs=4))
+        code_pool = ctx.enter_context(tc.tile_pool(name="code", bufs=5))
+        ost_pool = ctx.enter_context(tc.tile_pool(name="ost", bufs=8))
         psum = ctx.enter_context(tc.psum_pool(name="psum", bufs=8))
+        ctx.enter_context(tc.manual_schedule())
 
         ident = const.tile([P, P], F32, name="ident")
         make_identity(nc, ident[:])
         g_codes = const.tile([P, TOK_TILES, N_PASS * P], U32, name="g_codes", align_bytes=64)
         g_scales = const.tile([P, TOK_TILES, N_PASS * P], U8, name="g_scales", align_bytes=64)
 
+        chunks = [(r, c) for r in range(N_RANGES) for c in range(first_pass_of_range(r), N_PASS)]
+        n = len(chunks)
+        raws = {}
+        grps = {}
+        codes = {}
+        accs = {}
+
+        def copy_on(engine, dst, src):
+            if engine == "V":
+                nc.vector.tensor_copy(out=dst, in_=src)
+            else:
+                nc.scalar.copy(out=dst, in_=src)
+
+        def load(s):
+            r, c = chunks[s]
+            w, row0 = weight_rows(c)
+            raw = raw_pool.tile([P, 4, RANGE], BF16, name="raw", tag="raw")
+            for u in range(2):
+                rows = w[row0 + 256 * u : row0 + 256 * u + 256, RANGE * r : RANGE * r + RANGE]
+                nc.sync.dma_start(out=raw[:, 2 * u : 2 * u + 2, :], in_=rows.rearrange("(p e) w -> p e w", e=2))
+            raws[s] = raw
+
         g_raw = []
         for t in range(TOK_TILES):
             gr = graw_pool.tile([P, FEATURES], BF16, name="g_raw", tag="g_raw")
             nc.sync.dma_start(out=gr[:], in_=g[P * t : P * t + P, :])
             g_raw.append(gr)
+        for s in range(RAW_BUFS):
+            load(s)
 
         for t in range(TOK_TILES):
             words = g_raw[t][:].bitcast(F32)
@@ -75,83 +105,67 @@ def tile_naivematryoshkalinear_kernel(tc, x, W0, W1, W2, grad_out, out):
                     w0 = 512 * b + P * q
                     nc.tensor.transpose(xt[:, q, :], words[:, w0 : w0 + P], ident[:])
                 dst = grp_words[:, 512 * b : 512 * b + 512].rearrange("p (c r u) -> p c r u", c=2, u=2)
-                src = xt[:].rearrange("p (c u) r -> p c r u", u=2)
-                if b % 2 == 0:
-                    nc.vector.tensor_copy(out=dst, in_=src)
-                else:
-                    nc.scalar.copy(out=dst, in_=src)
+                copy_on(GCOPY[b], dst, xt[:].rearrange("p (c u) r -> p c r u", u=2))
             nc.vector.quantize_mx(
                 out=g_codes[:, t, :].bitcast(E5X4), scales=g_scales[:, t, :], in_=g_grp[:]
             )
 
-        chunks = [(r, c) for r in range(N_RANGES) for c in range(first_pass_of_range(r), N_PASS)]
-        n = len(chunks)
-        raws = {}
-        grps = {}
-        codes = {}
-        accs = {}
-
-        def load(s):
-            r, c = chunks[s]
-            w, row0 = weight_rows(c)
-            raw = raw_pool.tile([P, 4, RANGE], BF16, name="raw", tag="raw")
-            for u in range(2):
-                rows = w[row0 + 256 * u : row0 + 256 * u + 256, RANGE * r : RANGE * r + RANGE]
-                nc.sync.dma_start(out=raw[:, 2 * u : 2 * u + 2, :], in_=rows.rearrange("(p e) w -> p e w", e=2))
-            raws[s] = raw
-
         def regroup(s):
             raw = raws[s]
-            for j in range(2):
-                tag = "grp_v" if j == 0 else "grp_s"
-                grp = grp_pool.tile([P, BLOCK, 4], BF16, name=tag, tag=tag, align_bytes=64)
-                dst = grp[:].rearrange("p (c i) t -> p c t i", i=4)
-                src = raw[:, :, BLOCK * j : BLOCK * j + BLOCK].rearrange("p t (c i) -> p c t i", i=4)
-                if j == 0:
-                    nc.vector.tensor_copy(out=dst, in_=src)
-                else:
-                    nc.scalar.copy(out=dst, in_=src)
-                grps[(s, j)] = grp
+            grp = grp_pool.tile([P, RANGE, 4], BF16, name="grp", tag="grp", align_bytes=64)
+            nc.vector.tensor_copy(
+                out=grp[:, 0:VCOLS, :].rearrange("p (c i) t -> p c t i", i=4),
+                in_=raw[:, :, 0:VCOLS].rearrange("p t (c i) -> p c t i", i=4),
+            )
+            nc.scalar.copy(
+                out=grp[:, VCOLS:RANGE, :].rearrange("p (c i) t -> p c t i", i=4),
+                in_=raw[:, :, VCOLS:RANGE].rearrange("p t (c i) -> p c t i", i=4),
+            )
+            grps[s] = grp
 
         def quantise(s):
+            cw = code_pool.tile([P, RANGE], U32, name="w_codes", tag="w_codes", align_bytes=64)
+            cs = code_pool.tile([P, RANGE], U8, name="w_scales", tag="w_scales", align_bytes=64)
             for j in range(2):
-                cw = code_pool.tile([P, BLOCK], U32, name="w_codes", tag="w_codes", align_bytes=64)
-                cs = code_pool.tile([P, BLOCK], U8, name="w_scales", tag="w_scales", align_bytes=64)
                 nc.vector.quantize_mx(
-                    out=cw[:].bitcast(E4X4), scales=cs[:], in_=grps[(s, j)][:].rearrange("p w t -> p (w t)")
+                    out=cw[:, BLOCK * j : BLOCK * j + BLOCK].bitcast(E4X4),
+                    scales=cs[:, BLOCK * j : BLOCK * j + BLOCK],
+                    in_=grps[s][:, BLOCK * j : BLOCK * j + BLOCK, :].rearrange("p w t -> p (w t)"),
                 )
-                codes[(s, j)] = (cw, cs)
+            codes[s] = (cw, cs)
 
         def multiply(s):
             r, c = chunks[s]
             first = c == first_pass_of_range(r)
             last = c == N_PASS - 1
+            cw, cs = codes[s]
             for t in range(TOK_TILES):
                 for j in range(2):
                     if first:
                         accs[(t, j)] = psum.tile([P, BLOCK], F32, name="acc", tag="bank")
-                    cw, cs = codes[(s, j)]
                     nc.tensor.matmul_mx(
                         out=accs[(t, j)][:],
                         lhsT=g_codes[:, t, P * c : P * c + P].bitcast(E5X4),
                         lhsT_scale=g_scales[:, t, P * c : P * c + P],
-                        rhs=cw[:].bitcast(E4X4),
-                        rhs_scale=cs[:],
+                        rhs=cw[:, BLOCK * j : BLOCK * j + BLOCK].bitcast(E4X4),
+                        rhs_scale=cs[:, BLOCK * j : BLOCK * j + BLOCK],
                         start=first,
                         stop=last,
                     )
             if last:
+                pattern = EVAC_LAST if r == N_RANGES - 1 else EVAC
                 for t in range(TOK_TILES):
                     ost = ost_pool.tile([P, RANGE], F32, name="ost", tag="ost")
-                    nc.vector.tensor_copy(out=ost[:, 0:BLOCK], in_=accs[(t, 0)][:])
-                    nc.scalar.copy(out=ost[:, BLOCK:RANGE], in_=accs[(t, 1)][:])
+                    for j in range(2):
+                        copy_on(pattern[2 * t + j], ost[:, BLOCK * j : BLOCK * j + BLOCK], accs[(t, j)][:])
                     nc.sync.dma_start(out=o[P * t : P * t + P, RANGE * r : RANGE * r + RANGE], in_=ost[:])
 
         for s in range(n + 2):
             if s < n:
-                load(s)
                 regroup(s)
-            if 1 <= s <= n:
+            if s + RAW_BUFS < n:
+                load(s + RAW_BUFS)
+            if 1 <= s < n + 1:
                 quantise(s - 1)
             if s >= 2:
                 multiply(s - 2)

@@ -19,11 +19,11 @@ N_PASS = FEATURES // K_PASS
 BLOCK = 512
 RANGE = 1024
 N_RANGES = FEATURES // RANGE
-VCOLS = 608
-RAW_BUFS = 8
-EVAC = "SSSSSSSS"
-EVAC_LAST = "VSVSVSVS"
-GCOPY = "VSVS"
+RAW_BUFS = 10
+V_COLS = 512
+V_COLS_BUSY = 1024
+V_COLS_HALF = 320
+TAPER = 2
 
 FLOPS = 2 * TOKENS * (1024 * 1024 + 1024 * 2048 + 2048 * 4096)
 BYTES = 2 * (1024 * 1024 + 1024 * 2048 + 2048 * 4096) + 2 * TOKENS * FEATURES + 4 * TOKENS * FEATURES
@@ -51,11 +51,9 @@ def tile_naivematryoshkalinear_kernel(tc, x, W0, W1, W2, grad_out, out):
 
     with ExitStack() as ctx:
         const = ctx.enter_context(tc.tile_pool(name="const", bufs=1))
-        graw_pool = ctx.enter_context(tc.tile_pool(name="graw", bufs=4))
-        ggrp_pool = ctx.enter_context(tc.tile_pool(name="ggrp", bufs=2))
         raw_pool = ctx.enter_context(tc.tile_pool(name="raw", bufs=RAW_BUFS))
         grp_pool = ctx.enter_context(tc.tile_pool(name="grp", bufs=4))
-        code_pool = ctx.enter_context(tc.tile_pool(name="code", bufs=5))
+        code_pool = ctx.enter_context(tc.tile_pool(name="code", bufs=6))
         ost_pool = ctx.enter_context(tc.tile_pool(name="ost", bufs=8))
         psum = ctx.enter_context(tc.psum_pool(name="psum", bufs=8))
         ctx.enter_context(tc.manual_schedule())
@@ -67,6 +65,10 @@ def tile_naivematryoshkalinear_kernel(tc, x, W0, W1, W2, grad_out, out):
 
         chunks = [(r, c) for r in range(N_RANGES) for c in range(first_pass_of_range(r), N_PASS)]
         n = len(chunks)
+        units = [(s, (0, 1)) for s in range(n - TAPER)]
+        units += [(s, (j,)) for j in range(2) for s in range(n - TAPER, n)]
+        n_units = len(units)
+        busy_steps = [s + 2 for s in range(n) if chunks[s][1] == N_PASS - 1 and chunks[s][0] < N_RANGES - 1]
         raws = {}
         grps = {}
         codes = {}
@@ -87,17 +89,9 @@ def tile_naivematryoshkalinear_kernel(tc, x, W0, W1, W2, grad_out, out):
                 nc.sync.dma_start(out=raw[:, 2 * u : 2 * u + 2, :], in_=rows.rearrange("(p e) w -> p e w", e=2))
             raws[s] = raw
 
-        g_raw = []
-        for t in range(TOK_TILES):
-            gr = graw_pool.tile([P, FEATURES], BF16, name="g_raw", tag="g_raw")
-            nc.sync.dma_start(out=gr[:], in_=g[P * t : P * t + P, :])
-            g_raw.append(gr)
-        for s in range(RAW_BUFS):
-            load(s)
-
-        for t in range(TOK_TILES):
-            words = g_raw[t][:].bitcast(F32)
-            g_grp = ggrp_pool.tile([P, FEATURES], BF16, name="g_grp", tag="g_grp", align_bytes=64)
+        def quantise_tokens(t, g_raw):
+            words = g_raw[:].bitcast(F32)
+            g_grp = grp_pool.tile([P, FEATURES], BF16, name="g_grp", tag="grp", align_bytes=64)
             grp_words = g_grp[:].bitcast(F32)
             for b in range(4):
                 xt = psum.tile([P, 4, P], F32, name="xt", tag="bank")
@@ -105,67 +99,105 @@ def tile_naivematryoshkalinear_kernel(tc, x, W0, W1, W2, grad_out, out):
                     w0 = 512 * b + P * q
                     nc.tensor.transpose(xt[:, q, :], words[:, w0 : w0 + P], ident[:])
                 dst = grp_words[:, 512 * b : 512 * b + 512].rearrange("p (c r u) -> p c r u", c=2, u=2)
-                copy_on(GCOPY[b], dst, xt[:].rearrange("p (c u) r -> p c r u", u=2))
+                nc.scalar.copy(out=dst, in_=xt[:].rearrange("p (c u) r -> p c r u", u=2))
             nc.vector.quantize_mx(
                 out=g_codes[:, t, :].bitcast(E5X4), scales=g_scales[:, t, :], in_=g_grp[:]
             )
 
-        def regroup(s):
+        def regroup(i):
+            s, blocks = units[i]
             raw = raws[s]
-            grp = grp_pool.tile([P, RANGE, 4], BF16, name="grp", tag="grp", align_bytes=64)
+            cols = BLOCK * len(blocks)
+            base = BLOCK * blocks[0]
+            if len(blocks) == 1:
+                v_cols = V_COLS_HALF
+            elif s in busy_steps:
+                v_cols = V_COLS_BUSY
+            else:
+                v_cols = V_COLS
+            grp = grp_pool.tile([P, cols, 4], BF16, name="grp", tag="grp", align_bytes=64)
             nc.vector.tensor_copy(
-                out=grp[:, 0:VCOLS, :].rearrange("p (c i) t -> p c t i", i=4),
-                in_=raw[:, :, 0:VCOLS].rearrange("p t (c i) -> p c t i", i=4),
+                out=grp[:, 0:v_cols, :].rearrange("p (c i) t -> p c t i", i=4),
+                in_=raw[:, :, base : base + v_cols].rearrange("p t (c i) -> p c t i", i=4),
             )
-            nc.scalar.copy(
-                out=grp[:, VCOLS:RANGE, :].rearrange("p (c i) t -> p c t i", i=4),
-                in_=raw[:, :, VCOLS:RANGE].rearrange("p t (c i) -> p c t i", i=4),
-            )
-            grps[s] = grp
-
-        def quantise(s):
-            cw = code_pool.tile([P, RANGE], U32, name="w_codes", tag="w_codes", align_bytes=64)
-            cs = code_pool.tile([P, RANGE], U8, name="w_scales", tag="w_scales", align_bytes=64)
-            for j in range(2):
-                nc.vector.quantize_mx(
-                    out=cw[:, BLOCK * j : BLOCK * j + BLOCK].bitcast(E4X4),
-                    scales=cs[:, BLOCK * j : BLOCK * j + BLOCK],
-                    in_=grps[s][:, BLOCK * j : BLOCK * j + BLOCK, :].rearrange("p w t -> p (w t)"),
+            if v_cols < cols:
+                nc.scalar.copy(
+                    out=grp[:, v_cols:cols, :].rearrange("p (c i) t -> p c t i", i=4),
+                    in_=raw[:, :, base + v_cols : base + cols].rearrange("p t (c i) -> p c t i", i=4),
                 )
-            codes[s] = (cw, cs)
+            grps[i] = grp
 
-        def multiply(s):
+        def quantise(i):
+            s, blocks = units[i]
+            cols = BLOCK * len(blocks)
+            cw = code_pool.tile([P, cols], U32, name="w_codes", tag="w_codes", align_bytes=64)
+            cs = code_pool.tile([P, cols], U8, name="w_scales", tag="w_scales", align_bytes=64)
+            for k in range(len(blocks)):
+                part = slice(BLOCK * k, BLOCK * k + BLOCK)
+                nc.vector.quantize_mx(
+                    out=cw[:, part].bitcast(E4X4),
+                    scales=cs[:, part],
+                    in_=grps[i][:, part, :].rearrange("p w t -> p (w t)"),
+                )
+                codes[(s, blocks[k])] = (cw[:, part], cs[:, part])
+
+        def multiply(i):
+            s, blocks = units[i]
             r, c = chunks[s]
             first = c == first_pass_of_range(r)
             last = c == N_PASS - 1
-            cw, cs = codes[s]
             for t in range(TOK_TILES):
-                for j in range(2):
+                for j in blocks:
                     if first:
                         accs[(t, j)] = psum.tile([P, BLOCK], F32, name="acc", tag="bank")
+                    cw, cs = codes[(s, j)]
                     nc.tensor.matmul_mx(
                         out=accs[(t, j)][:],
                         lhsT=g_codes[:, t, P * c : P * c + P].bitcast(E5X4),
                         lhsT_scale=g_scales[:, t, P * c : P * c + P],
-                        rhs=cw[:, BLOCK * j : BLOCK * j + BLOCK].bitcast(E4X4),
-                        rhs_scale=cs[:, BLOCK * j : BLOCK * j + BLOCK],
+                        rhs=cw.bitcast(E4X4),
+                        rhs_scale=cs,
                         start=first,
                         stop=last,
                     )
-            if last:
-                pattern = EVAC_LAST if r == N_RANGES - 1 else EVAC
+            if not last:
+                return
+            if len(blocks) == 2:
                 for t in range(TOK_TILES):
                     ost = ost_pool.tile([P, RANGE], F32, name="ost", tag="ost")
-                    for j in range(2):
-                        copy_on(pattern[2 * t + j], ost[:, BLOCK * j : BLOCK * j + BLOCK], accs[(t, j)][:])
+                    for j in blocks:
+                        nc.scalar.copy(out=ost[:, BLOCK * j : BLOCK * j + BLOCK], in_=accs[(t, j)][:])
                     nc.sync.dma_start(out=o[P * t : P * t + P, RANGE * r : RANGE * r + RANGE], in_=ost[:])
+            else:
+                j = blocks[0]
+                col0 = RANGE * r + BLOCK * j
+                for t in range(TOK_TILES):
+                    ost = ost_pool.tile([P, BLOCK], F32, name="ost_half", tag="ost")
+                    copy_on("V" if j == 1 and t % 2 == 0 else "S", ost[:], accs[(t, j)][:])
+                    nc.sync.dma_start(out=o[P * t : P * t + P, col0 : col0 + BLOCK], in_=ost[:])
 
-        for s in range(n + 2):
-            if s < n:
-                regroup(s)
-            if s + RAW_BUFS < n:
-                load(s + RAW_BUFS)
-            if 1 <= s < n + 1:
-                quantise(s - 1)
-            if s >= 2:
-                multiply(s - 2)
+        g_raws = []
+        for t in range(TOK_TILES):
+            g_raw = raw_pool.tile([P, FEATURES], BF16, name="g_raw", tag="raw")
+            nc.sync.dma_start(out=g_raw[:], in_=g[P * t : P * t + P, :])
+            g_raws.append(g_raw)
+        loaded = 0
+        for k in range(TOK_TILES, RAW_BUFS):
+            load(loaded)
+            loaded += 1
+        for t in range(TOK_TILES):
+            quantise_tokens(t, g_raws[t])
+            load(loaded)
+            loaded += 1
+
+        for step in range(n_units + 2):
+            if step < n_units:
+                regroup(step)
+                s, blocks = units[step]
+                if blocks[-1] == 1 and loaded < n:
+                    load(loaded)
+                    loaded += 1
+            if 1 <= step <= n_units:
+                quantise(step - 1)
+            if step >= 2:
+                multiply(step - 2)

@@ -19,22 +19,19 @@ N_PASS = FEATURES // K_PASS
 BLOCK = 512
 RANGE = 1024
 N_RANGES = FEATURES // RANGE
-RAW_BUFS = 10
+RAW_BUFS = 5
 V_COLS = 512
 V_COLS_BUSY = 1024
 V_COLS_HALF = 320
 TAPER = 2
+PASSES_PER_STEP = 16
+GROUPS = [
+    ("stack", 0, 0), ("stack", 4, 0), ("stack", 6, 0), ("pair", 2, 0), ("pair", 3, 0),
+    ("stack", 4, 1), ("stack", 6, 1), ("stack", 4, 2), ("stack", 6, 2), ("stack", 4, 3), ("stack", 6, 3),
+]
 
 FLOPS = 2 * TOKENS * (1024 * 1024 + 1024 * 2048 + 2048 * 4096)
 BYTES = 2 * (1024 * 1024 + 1024 * 2048 + 2048 * 4096) + 2 * TOKENS * FEATURES + 4 * TOKENS * FEATURES
-
-
-def first_pass_of_range(r):
-    if r == 0:
-        return 0
-    if r == 1:
-        return 2
-    return 4
 
 
 def tile_naivematryoshkalinear_kernel(tc, x, W0, W1, W2, grad_out, out):
@@ -54,7 +51,8 @@ def tile_naivematryoshkalinear_kernel(tc, x, W0, W1, W2, grad_out, out):
         raw_pool = ctx.enter_context(tc.tile_pool(name="raw", bufs=RAW_BUFS))
         grp_pool = ctx.enter_context(tc.tile_pool(name="grp", bufs=4))
         code_pool = ctx.enter_context(tc.tile_pool(name="code", bufs=6))
-        ost_pool = ctx.enter_context(tc.tile_pool(name="ost", bufs=8))
+        ost_pool = ctx.enter_context(tc.tile_pool(name="ost", bufs=6))
+        wide_pool = ctx.enter_context(tc.tile_pool(name="wide", bufs=TOK_TILES))
         psum = ctx.enter_context(tc.psum_pool(name="psum", bufs=8))
         ctx.enter_context(tc.manual_schedule())
 
@@ -63,16 +61,29 @@ def tile_naivematryoshkalinear_kernel(tc, x, W0, W1, W2, grad_out, out):
         g_codes = const.tile([P, TOK_TILES, N_PASS * P], U32, name="g_codes", align_bytes=64)
         g_scales = const.tile([P, TOK_TILES, N_PASS * P], U8, name="g_scales", align_bytes=64)
 
-        chunks = [(r, c) for r in range(N_RANGES) for c in range(first_pass_of_range(r), N_PASS)]
+        chunks = []
+        for gi in range(len(GROUPS)):
+            kind, c, r = GROUPS[gi]
+            for h in range(2):
+                chunks.append((c + h, r, gi, h) if kind == "stack" else (c, r + h, gi, h))
         n = len(chunks)
         units = [(s, (0, 1)) for s in range(n - TAPER)]
         units += [(s, (j,)) for j in range(2) for s in range(n - TAPER, n)]
         n_units = len(units)
-        busy_steps = [s + 2 for s in range(n) if chunks[s][1] == N_PASS - 1 and chunks[s][0] < N_RANGES - 1]
+        pe_order = [i for r in range(N_RANGES) for i in range(n_units) if chunks[units[i][0]][1] == r]
+        opens = {}
+        closes = {}
+        for i in pe_order:
+            r = chunks[units[i][0]][1]
+            for j in units[i][1]:
+                if (r, j) not in opens:
+                    opens[(r, j)] = i
+                closes[(r, j)] = i
         raws = {}
         grps = {}
         codes = {}
         accs = {}
+        wides = {}
 
         def copy_on(engine, dst, src):
             if engine == "V":
@@ -80,38 +91,47 @@ def tile_naivematryoshkalinear_kernel(tc, x, W0, W1, W2, grad_out, out):
             else:
                 nc.scalar.copy(out=dst, in_=src)
 
-        def load(s):
-            r, c = chunks[s]
-            w, row0 = weight_rows(c)
-            raw = raw_pool.tile([P, 4, RANGE], BF16, name="raw", tag="raw")
-            for u in range(2):
-                rows = w[row0 + 256 * u : row0 + 256 * u + 256, RANGE * r : RANGE * r + RANGE]
-                nc.sync.dma_start(out=raw[:, 2 * u : 2 * u + 2, :], in_=rows.rearrange("(p e) w -> p e w", e=2))
-            raws[s] = raw
+        def load(gi):
+            kind, c, r = GROUPS[gi]
+            if kind == "stack":
+                raw = raw_pool.tile([P, 2, 4, RANGE], BF16, name="raw", tag="raw")
+                for h in range(2):
+                    w, row0 = weight_rows(c + h)
+                    rows = w[row0 : row0 + K_PASS, RANGE * r : RANGE * r + RANGE]
+                    nc.sync.dma_start(out=raw[:, h, :, :], in_=rows.rearrange("(p t) w -> p t w", t=4))
+                    raws[(gi, h)] = raw[:, h, :, :]
+            else:
+                raw = raw_pool.tile([P, 4, 2 * RANGE], BF16, name="raw_pair", tag="raw")
+                w, row0 = weight_rows(c)
+                rows = w[row0 : row0 + K_PASS, RANGE * r : RANGE * r + 2 * RANGE]
+                nc.sync.dma_start(out=raw[:], in_=rows.rearrange("(p t) w -> p t w", t=4))
+                for h in range(2):
+                    raws[(gi, h)] = raw[:, :, RANGE * h : RANGE * h + RANGE]
 
         def quantise_tokens(t, g_raw):
-            words = g_raw[:].bitcast(F32)
+            words = g_raw.bitcast(F32)
             g_grp = grp_pool.tile([P, FEATURES], BF16, name="g_grp", tag="grp", align_bytes=64)
             grp_words = g_grp[:].bitcast(F32)
             for b in range(4):
                 xt = psum.tile([P, 4, P], F32, name="xt", tag="bank")
                 for q in range(4):
-                    w0 = 512 * b + P * q
-                    nc.tensor.transpose(xt[:, q, :], words[:, w0 : w0 + P], ident[:])
+                    c = 2 * b + q // 2
+                    pass_words = words[:, 256 * c : 256 * c + 256].rearrange("r (p u) -> r u p", u=2)
+                    nc.tensor.transpose(xt[:, q, :], pass_words[:, q % 2, :], ident[:])
                 dst = grp_words[:, 512 * b : 512 * b + 512].rearrange("p (c r u) -> p c r u", c=2, u=2)
                 nc.scalar.copy(out=dst, in_=xt[:].rearrange("p (c u) r -> p c r u", u=2))
             nc.vector.quantize_mx(
                 out=g_codes[:, t, :].bitcast(E5X4), scales=g_scales[:, t, :], in_=g_grp[:]
             )
 
-        def regroup(i):
+        def regroup(i, scalar_is_busy):
             s, blocks = units[i]
-            raw = raws[s]
+            raw = raws[(chunks[s][2], chunks[s][3])]
             cols = BLOCK * len(blocks)
             base = BLOCK * blocks[0]
             if len(blocks) == 1:
                 v_cols = V_COLS_HALF
-            elif s in busy_steps:
+            elif scalar_is_busy:
                 v_cols = V_COLS_BUSY
             else:
                 v_cols = V_COLS
@@ -139,65 +159,96 @@ def tile_naivematryoshkalinear_kernel(tc, x, W0, W1, W2, grad_out, out):
                     scales=cs[:, part],
                     in_=grps[i][:, part, :].rearrange("p w t -> p (w t)"),
                 )
-                codes[(s, blocks[k])] = (cw[:, part], cs[:, part])
+                codes[(i, blocks[k])] = (cw[:, part], cs[:, part])
 
         def multiply(i):
             s, blocks = units[i]
-            r, c = chunks[s]
-            first = c == first_pass_of_range(r)
-            last = c == N_PASS - 1
+            c, r = chunks[s][0], chunks[s][1]
             for t in range(TOK_TILES):
                 for j in blocks:
-                    if first:
+                    if opens[(r, j)] == i:
                         accs[(t, j)] = psum.tile([P, BLOCK], F32, name="acc", tag="bank")
-                    cw, cs = codes[(s, j)]
+                    cw, cs = codes[(i, j)]
                     nc.tensor.matmul_mx(
                         out=accs[(t, j)][:],
                         lhsT=g_codes[:, t, P * c : P * c + P].bitcast(E5X4),
                         lhsT_scale=g_scales[:, t, P * c : P * c + P],
                         rhs=cw.bitcast(E4X4),
                         rhs_scale=cs,
-                        start=first,
-                        stop=last,
+                        start=opens[(r, j)] == i,
+                        stop=closes[(r, j)] == i,
                     )
-            if not last:
+            if closes[(r, blocks[0])] != i:
                 return
-            if len(blocks) == 2:
+            rows = [slice(P * t, P * t + P) for t in range(TOK_TILES)]
+            if r < 2:
+                for t in range(TOK_TILES):
+                    if r == 0:
+                        wides[t] = wide_pool.tile([P, 2 * RANGE], F32, name="wide", tag="wide")
+                    for j in blocks:
+                        col0 = RANGE * r + BLOCK * j
+                        nc.scalar.copy(out=wides[t][:, col0 : col0 + BLOCK], in_=accs[(t, j)][:])
+                    if r == 1:
+                        nc.sync.dma_start(out=o[rows[t], 0 : 2 * RANGE], in_=wides[t][:])
+            elif len(blocks) == 2:
                 for t in range(TOK_TILES):
                     ost = ost_pool.tile([P, RANGE], F32, name="ost", tag="ost")
                     for j in blocks:
                         nc.scalar.copy(out=ost[:, BLOCK * j : BLOCK * j + BLOCK], in_=accs[(t, j)][:])
-                    nc.sync.dma_start(out=o[P * t : P * t + P, RANGE * r : RANGE * r + RANGE], in_=ost[:])
+                    nc.sync.dma_start(out=o[rows[t], RANGE * r : RANGE * r + RANGE], in_=ost[:])
             else:
                 j = blocks[0]
                 col0 = RANGE * r + BLOCK * j
                 for t in range(TOK_TILES):
                     ost = ost_pool.tile([P, BLOCK], F32, name="ost_half", tag="ost")
                     copy_on("V" if j == 1 and t % 2 == 0 else "S", ost[:], accs[(t, j)][:])
-                    nc.sync.dma_start(out=o[P * t : P * t + P, col0 : col0 + BLOCK], in_=ost[:])
+                    nc.sync.dma_start(out=o[rows[t], col0 : col0 + BLOCK], in_=ost[:])
 
         g_raws = []
-        for t in range(TOK_TILES):
-            g_raw = raw_pool.tile([P, FEATURES], BF16, name="g_raw", tag="raw")
-            nc.sync.dma_start(out=g_raw[:], in_=g[P * t : P * t + P, :])
-            g_raws.append(g_raw)
+        for k in range(TOK_TILES // 2):
+            g_raw = raw_pool.tile([P, 2, FEATURES], BF16, name="g_raw", tag="raw")
+            for h in range(2):
+                t = 2 * k + h
+                nc.sync.dma_start(out=g_raw[:, h, :], in_=g[P * t : P * t + P, :])
+                g_raws.append(g_raw[:, h, :])
         loaded = 0
-        for k in range(TOK_TILES, RAW_BUFS):
+        for k in range(TOK_TILES // 2, RAW_BUFS):
             load(loaded)
             loaded += 1
         for t in range(TOK_TILES):
             quantise_tokens(t, g_raws[t])
-            load(loaded)
-            loaded += 1
+            if t % 2 == 1:
+                load(loaded)
+                loaded += 1
 
-        for step in range(n_units + 2):
+        last_unit_of_group = {}
+        for i in range(n_units):
+            last_unit_of_group[chunks[units[i][0]][2]] = i
+        issued = 0
+        step = 0
+        while issued < n_units:
+            todo = []
+            room = PASSES_PER_STEP
+            while issued + len(todo) < n_units:
+                i = pe_order[issued + len(todo)]
+                passes = TOK_TILES * len(units[i][1])
+                if i > step - 2 or passes > room:
+                    break
+                todo.append(i)
+                room -= passes
+            scalar_is_busy = False
+            for i in todo:
+                r = chunks[units[i][0]][1]
+                if len(units[i][1]) == 2 and closes[(r, 0)] == i:
+                    scalar_is_busy = True
             if step < n_units:
-                regroup(step)
-                s, blocks = units[step]
-                if blocks[-1] == 1 and loaded < n:
+                regroup(step, scalar_is_busy)
+                if last_unit_of_group[chunks[units[step][0]][2]] == step and loaded < len(GROUPS):
                     load(loaded)
                     loaded += 1
             if 1 <= step <= n_units:
                 quantise(step - 1)
-            if step >= 2:
-                multiply(step - 2)
+            for i in todo:
+                multiply(i)
+            issued += len(todo)
+            step += 1

@@ -23,8 +23,10 @@ RAW_BUFS = 5
 V_COLS = 512
 V_COLS_BUSY = 1024
 V_COLS_HALF = 320
+V_COLS_HEAD = 704
 TAPER = 2
 PASSES_PER_STEP = 16
+TRANSPOSE_BANKS = [[2, 3, 4, 5], [4, 5, 6, 7], [6, 7, 6, 7], [6, 7, 6, 7]]
 GROUPS = [
     ("stack", 0, 0), ("stack", 4, 0), ("stack", 6, 0), ("pair", 2, 0), ("pair", 3, 0),
     ("stack", 4, 1), ("stack", 6, 1), ("stack", 4, 2), ("stack", 6, 2), ("stack", 4, 3), ("stack", 6, 3),
@@ -53,7 +55,7 @@ def tile_naivematryoshkalinear_kernel(tc, x, W0, W1, W2, grad_out, out):
         code_pool = ctx.enter_context(tc.tile_pool(name="code", bufs=6))
         ost_pool = ctx.enter_context(tc.tile_pool(name="ost", bufs=6))
         wide_pool = ctx.enter_context(tc.tile_pool(name="wide", bufs=TOK_TILES))
-        psum = ctx.enter_context(tc.psum_pool(name="psum", bufs=8))
+        psum = ctx.enter_context(tc.psum_pool(name="psum", bufs=1))
         ctx.enter_context(tc.manual_schedule())
 
         ident = const.tile([P, P], F32, name="ident")
@@ -84,6 +86,7 @@ def tile_naivematryoshkalinear_kernel(tc, x, W0, W1, W2, grad_out, out):
         codes = {}
         accs = {}
         wides = {}
+        g_grps = {}
 
         def copy_on(engine, dst, src):
             if engine == "V":
@@ -91,15 +94,19 @@ def tile_naivematryoshkalinear_kernel(tc, x, W0, W1, W2, grad_out, out):
             else:
                 nc.scalar.copy(out=dst, in_=src)
 
+        def load_stack_half(gi, h, raw):
+            kind, c, r = GROUPS[gi]
+            w, row0 = weight_rows(c + h)
+            rows = w[row0 : row0 + K_PASS, RANGE * r : RANGE * r + RANGE]
+            nc.sync.dma_start(out=raw[:, h, :, :], in_=rows.rearrange("(p t) w -> p t w", t=4))
+            raws[(gi, h)] = raw[:, h, :, :]
+
         def load(gi):
             kind, c, r = GROUPS[gi]
             if kind == "stack":
                 raw = raw_pool.tile([P, 2, 4, RANGE], BF16, name="raw", tag="raw")
                 for h in range(2):
-                    w, row0 = weight_rows(c + h)
-                    rows = w[row0 : row0 + K_PASS, RANGE * r : RANGE * r + RANGE]
-                    nc.sync.dma_start(out=raw[:, h, :, :], in_=rows.rearrange("(p t) w -> p t w", t=4))
-                    raws[(gi, h)] = raw[:, h, :, :]
+                    load_stack_half(gi, h, raw)
             else:
                 raw = raw_pool.tile([P, 4, 2 * RANGE], BF16, name="raw_pair", tag="raw")
                 w, row0 = weight_rows(c)
@@ -108,23 +115,26 @@ def tile_naivematryoshkalinear_kernel(tc, x, W0, W1, W2, grad_out, out):
                 for h in range(2):
                     raws[(gi, h)] = raw[:, :, RANGE * h : RANGE * h + RANGE]
 
-        def quantise_tokens(t, g_raw):
+        def transpose_tokens(t, g_raw):
             words = g_raw.bitcast(F32)
             g_grp = grp_pool.tile([P, FEATURES], BF16, name="g_grp", tag="grp", align_bytes=64)
+            g_grps[t] = g_grp
             grp_words = g_grp[:].bitcast(F32)
             for b in range(4):
-                xt = psum.tile([P, 4, P], F32, name="xt", tag="bank")
+                xt = psum.tile([P, 4, P], F32, name="xt", tag="bank%d" % TRANSPOSE_BANKS[t][b])
                 for q in range(4):
                     c = 2 * b + q // 2
                     pass_words = words[:, 256 * c : 256 * c + 256].rearrange("r (p u) -> r u p", u=2)
                     nc.tensor.transpose(xt[:, q, :], pass_words[:, q % 2, :], ident[:])
                 dst = grp_words[:, 512 * b : 512 * b + 512].rearrange("p (c r u) -> p c r u", c=2, u=2)
                 nc.scalar.copy(out=dst, in_=xt[:].rearrange("p (c u) r -> p c r u", u=2))
+
+        def quantise_tokens(t):
             nc.vector.quantize_mx(
-                out=g_codes[:, t, :].bitcast(E5X4), scales=g_scales[:, t, :], in_=g_grp[:]
+                out=g_codes[:, t, :].bitcast(E5X4), scales=g_scales[:, t, :], in_=g_grps[t][:]
             )
 
-        def regroup(i, scalar_is_busy):
+        def regroup(i, scalar_is_busy, in_head):
             s, blocks = units[i]
             raw = raws[(chunks[s][2], chunks[s][3])]
             cols = BLOCK * len(blocks)
@@ -133,6 +143,8 @@ def tile_naivematryoshkalinear_kernel(tc, x, W0, W1, W2, grad_out, out):
                 v_cols = V_COLS_HALF
             elif scalar_is_busy:
                 v_cols = V_COLS_BUSY
+            elif in_head:
+                v_cols = V_COLS_HEAD
             else:
                 v_cols = V_COLS
             grp = grp_pool.tile([P, cols, 4], BF16, name="grp", tag="grp", align_bytes=64)
@@ -161,94 +173,119 @@ def tile_naivematryoshkalinear_kernel(tc, x, W0, W1, W2, grad_out, out):
                 )
                 codes[(i, blocks[k])] = (cw[:, part], cs[:, part])
 
-        def multiply(i):
+        def multiply(i, t):
             s, blocks = units[i]
             c, r = chunks[s][0], chunks[s][1]
-            for t in range(TOK_TILES):
-                for j in blocks:
-                    if opens[(r, j)] == i:
-                        accs[(t, j)] = psum.tile([P, BLOCK], F32, name="acc", tag="bank")
-                    cw, cs = codes[(i, j)]
-                    nc.tensor.matmul_mx(
-                        out=accs[(t, j)][:],
-                        lhsT=g_codes[:, t, P * c : P * c + P].bitcast(E5X4),
-                        lhsT_scale=g_scales[:, t, P * c : P * c + P],
-                        rhs=cw.bitcast(E4X4),
-                        rhs_scale=cs,
-                        start=opens[(r, j)] == i,
-                        stop=closes[(r, j)] == i,
-                    )
+            for j in blocks:
+                if opens[(r, j)] == i:
+                    accs[(t, j)] = psum.tile([P, BLOCK], F32, name="acc", tag="bank%d" % (2 * t + j))
+                cw, cs = codes[(i, j)]
+                nc.tensor.matmul_mx(
+                    out=accs[(t, j)][:],
+                    lhsT=g_codes[:, t, P * c : P * c + P].bitcast(E5X4),
+                    lhsT_scale=g_scales[:, t, P * c : P * c + P],
+                    rhs=cw.bitcast(E4X4),
+                    rhs_scale=cs,
+                    start=opens[(r, j)] == i,
+                    stop=closes[(r, j)] == i,
+                )
             if closes[(r, blocks[0])] != i:
                 return
-            rows = [slice(P * t, P * t + P) for t in range(TOK_TILES)]
+            rows = slice(P * t, P * t + P)
             if r < 2:
-                for t in range(TOK_TILES):
-                    if r == 0:
-                        wides[t] = wide_pool.tile([P, 2 * RANGE], F32, name="wide", tag="wide")
-                    for j in blocks:
-                        col0 = RANGE * r + BLOCK * j
-                        nc.scalar.copy(out=wides[t][:, col0 : col0 + BLOCK], in_=accs[(t, j)][:])
-                    if r == 1:
-                        nc.sync.dma_start(out=o[rows[t], 0 : 2 * RANGE], in_=wides[t][:])
+                if r == 0:
+                    wides[t] = wide_pool.tile([P, 2 * RANGE], F32, name="wide", tag="wide")
+                for j in blocks:
+                    col0 = RANGE * r + BLOCK * j
+                    nc.scalar.copy(out=wides[t][:, col0 : col0 + BLOCK], in_=accs[(t, j)][:])
+                if r == 1:
+                    nc.sync.dma_start(out=o[rows, 0 : 2 * RANGE], in_=wides[t][:])
             elif len(blocks) == 2:
-                for t in range(TOK_TILES):
-                    ost = ost_pool.tile([P, RANGE], F32, name="ost", tag="ost")
-                    for j in blocks:
-                        nc.scalar.copy(out=ost[:, BLOCK * j : BLOCK * j + BLOCK], in_=accs[(t, j)][:])
-                    nc.sync.dma_start(out=o[rows[t], RANGE * r : RANGE * r + RANGE], in_=ost[:])
+                ost = ost_pool.tile([P, RANGE], F32, name="ost", tag="ost")
+                for j in blocks:
+                    nc.scalar.copy(out=ost[:, BLOCK * j : BLOCK * j + BLOCK], in_=accs[(t, j)][:])
+                nc.sync.dma_start(out=o[rows, RANGE * r : RANGE * r + RANGE], in_=ost[:])
             else:
                 j = blocks[0]
                 col0 = RANGE * r + BLOCK * j
-                for t in range(TOK_TILES):
-                    ost = ost_pool.tile([P, BLOCK], F32, name="ost_half", tag="ost")
-                    copy_on("V" if j == 1 and t % 2 == 0 else "S", ost[:], accs[(t, j)][:])
-                    nc.sync.dma_start(out=o[rows[t], col0 : col0 + BLOCK], in_=ost[:])
+                ost = ost_pool.tile([P, BLOCK], F32, name="ost_half", tag="ost")
+                copy_on("V" if j == 1 and t % 2 == 0 else "S", ost[:], accs[(t, j)][:])
+                nc.sync.dma_start(out=o[rows, col0 : col0 + BLOCK], in_=ost[:])
 
         g_raws = []
         for k in range(TOK_TILES // 2):
             g_raw = raw_pool.tile([P, 2, FEATURES], BF16, name="g_raw", tag="raw")
+            w_raw = raw_pool.tile([P, 2, 4, RANGE], BF16, name="raw", tag="raw")
             for h in range(2):
                 t = 2 * k + h
                 nc.sync.dma_start(out=g_raw[:, h, :], in_=g[P * t : P * t + P, :])
                 g_raws.append(g_raw[:, h, :])
-        loaded = 0
-        for k in range(TOK_TILES // 2, RAW_BUFS):
+                load_stack_half(k, h, w_raw)
+        loaded = TOK_TILES // 2
+        for k in range(TOK_TILES, RAW_BUFS):
             load(loaded)
             loaded += 1
+
+        work = []
         for t in range(TOK_TILES):
-            quantise_tokens(t, g_raws[t])
-            if t % 2 == 1:
-                load(loaded)
-                loaded += 1
+            work += [("g", t), ("u", t)]
+        work += [("u", i) for i in range(TOK_TILES, n_units)]
+        n_work = len(work)
+        ready_g = {}
+        ready_u = {}
+        for w in range(n_work):
+            if work[w][0] == "g":
+                ready_g[work[w][1]] = w + 2
+            else:
+                ready_u[work[w][1]] = w + 2
+
+        def ready(product):
+            return max(ready_u[product[0]], ready_g[product[1]])
+
+        pe_seq = []
+        for r in range(N_RANGES):
+            products = [(i, t) for i in pe_order if chunks[units[i][0]][1] == r for t in range(TOK_TILES)]
+            pe_seq += sorted(products, key=lambda pr: (ready(pr), pe_order.index(pr[0]), pr[1]))
 
         last_unit_of_group = {}
         for i in range(n_units):
             last_unit_of_group[chunks[units[i][0]][2]] = i
         issued = 0
         step = 0
-        while issued < n_units:
+        while issued < len(pe_seq):
             todo = []
             room = PASSES_PER_STEP
-            while issued + len(todo) < n_units:
-                i = pe_order[issued + len(todo)]
-                passes = TOK_TILES * len(units[i][1])
-                if i > step - 2 or passes > room:
+            while issued + len(todo) < len(pe_seq):
+                product = pe_seq[issued + len(todo)]
+                passes = len(units[product[0]][1])
+                if ready(product) > step or passes > room:
                     break
-                todo.append(i)
+                todo.append(product)
                 room -= passes
             scalar_is_busy = False
-            for i in todo:
+            for i, t in todo:
                 r = chunks[units[i][0]][1]
                 if len(units[i][1]) == 2 and closes[(r, 0)] == i:
                     scalar_is_busy = True
-            if step < n_units:
-                regroup(step, scalar_is_busy)
-                if last_unit_of_group[chunks[units[step][0]][2]] == step and loaded < len(GROUPS):
+            if step < n_work:
+                kind, a = work[step]
+                frees_a_slot = False
+                if kind == "g":
+                    transpose_tokens(a, g_raws[a])
+                    frees_a_slot = a % 2 == 1
+                else:
+                    regroup(a, scalar_is_busy, step < 2 * TOK_TILES)
+                    frees_a_slot = last_unit_of_group[chunks[units[a][0]][2]] == a
+                if frees_a_slot and loaded < len(GROUPS):
                     load(loaded)
                     loaded += 1
-            if 1 <= step <= n_units:
-                quantise(step - 1)
-            for i in todo:
-                multiply(i)
+            if 1 <= step <= n_work:
+                kind, a = work[step - 1]
+                if kind == "g":
+                    quantise_tokens(a)
+                else:
+                    quantise(a)
+            for i, t in todo:
+                multiply(i, t)
             issued += len(todo)
             step += 1

@@ -149,13 +149,13 @@ def tile_naivematryoshkalinear_kernel(tc, x, W0, W1, W2, grad_out, out):
                 v_cols = V_COLS
             grp = grp_pool.tile([P, cols, 4], BF16, name="grp", tag="grp", align_bytes=64)
             nc.vector.tensor_copy(
-                out=grp[:, 0:v_cols, :].rearrange("p (c i) t -> p c t i", i=4),
-                in_=raw[:, :, base : base + v_cols].rearrange("p t (c i) -> p c t i", i=4),
+                out=grp[:, 0:v_cols, :].rearrange("p (c i) t -> p c t i", i=8),
+                in_=raw[:, :, base : base + v_cols].rearrange("p t (c i) -> p c t i", i=8),
             )
             if v_cols < cols:
                 nc.scalar.copy(
-                    out=grp[:, v_cols:cols, :].rearrange("p (c i) t -> p c t i", i=4),
-                    in_=raw[:, :, base + v_cols : base + cols].rearrange("p t (c i) -> p c t i", i=4),
+                    out=grp[:, v_cols:cols, :].rearrange("p (c i) t -> p c t i", i=8),
+                    in_=raw[:, :, base + v_cols : base + cols].rearrange("p t (c i) -> p c t i", i=8),
                 )
             grps[i] = grp
 

@@ -19,17 +19,27 @@ N_PASS = FEATURES // K_PASS
 BLOCK = 512
 RANGE = 1024
 N_RANGES = FEATURES // RANGE
-RAW_BUFS = 5
+RUN = 8
 V_COLS = 512
-V_COLS_BUSY = 1024
-V_COLS_HALF = 320
+V_COLS_PER_BANK = 64
 V_COLS_HEAD = 704
+V_COLS_HALF = 320
 TAPER = 2
-PASSES_PER_STEP = 16
+PASSES_PER_STEP = 12
+RAW_SINGLES = 6
+RAW_PAIRS = 3
+CODE_BUFS = 6
 TRANSPOSE_BANKS = [[2, 3, 4, 5], [4, 5, 6, 7], [6, 7, 6, 7], [6, 7, 6, 7]]
-GROUPS = [
-    ("stack", 0, 0), ("stack", 4, 0), ("stack", 6, 0), ("pair", 2, 0), ("pair", 3, 0),
-    ("stack", 4, 1), ("stack", 6, 1), ("stack", 4, 2), ("stack", 6, 2), ("stack", 4, 3), ("stack", 6, 3),
+LOADS = [
+    ("g", 0), ("w", 0, 0), ("g", 1), ("w", 1, 0), ("g", 2), ("w", 4, 0), ("g", 3), ("w", 5, 0),
+    ("w", 6, 0), ("w", 7, 0), ("p", 2, 0), ("p", 3, 0), ("w", 4, 1), ("w", 5, 1), ("p", 6, 1), ("p",
+    7, 1), ("p", 4, 2), ("p", 5, 2), ("w", 6, 3), ("w", 7, 3),
+]
+ORDER = [
+    ("g", 0), ("w", 0, 0), ("g", 1), ("w", 1, 0), ("g", 2), ("w", 4, 0), ("g", 3), ("w", 5, 0),
+    ("w", 6, 0), ("w", 7, 0), ("w", 2, 0), ("w", 2, 1), ("w", 3, 0), ("w", 3, 1), ("w", 4, 1), ("w",
+    5, 1), ("w", 6, 1), ("w", 6, 2), ("w", 7, 1), ("w", 7, 2), ("w", 4, 2), ("w", 4, 3), ("w", 5,
+    2), ("w", 5, 3), ("w", 6, 3), ("w", 7, 3),
 ]
 
 FLOPS = 2 * TOKENS * (1024 * 1024 + 1024 * 2048 + 2048 * 4096)
@@ -50,9 +60,10 @@ def tile_naivematryoshkalinear_kernel(tc, x, W0, W1, W2, grad_out, out):
 
     with ExitStack() as ctx:
         const = ctx.enter_context(tc.tile_pool(name="const", bufs=1))
-        raw_pool = ctx.enter_context(tc.tile_pool(name="raw", bufs=RAW_BUFS))
+        raw_pool = ctx.enter_context(tc.tile_pool(name="raw", bufs=RAW_SINGLES))
+        raw2_pool = ctx.enter_context(tc.tile_pool(name="raw2", bufs=RAW_PAIRS))
         grp_pool = ctx.enter_context(tc.tile_pool(name="grp", bufs=4))
-        code_pool = ctx.enter_context(tc.tile_pool(name="code", bufs=6))
+        code_pool = ctx.enter_context(tc.tile_pool(name="code", bufs=CODE_BUFS))
         ost_pool = ctx.enter_context(tc.tile_pool(name="ost", bufs=6))
         wide_pool = ctx.enter_context(tc.tile_pool(name="wide", bufs=TOK_TILES))
         psum = ctx.enter_context(tc.psum_pool(name="psum", bufs=1))
@@ -63,30 +74,22 @@ def tile_naivematryoshkalinear_kernel(tc, x, W0, W1, W2, grad_out, out):
         g_codes = const.tile([P, TOK_TILES, N_PASS * P], U32, name="g_codes", align_bytes=64)
         g_scales = const.tile([P, TOK_TILES, N_PASS * P], U8, name="g_scales", align_bytes=64)
 
-        chunks = []
-        for gi in range(len(GROUPS)):
-            kind, c, r = GROUPS[gi]
-            for h in range(2):
-                chunks.append((c + h, r, gi, h) if kind == "stack" else (c, r + h, gi, h))
+        chunks = [(w[1], w[2]) for w in ORDER if w[0] == "w"]
         n = len(chunks)
-        units = [(s, (0, 1)) for s in range(n - TAPER)]
-        units += [(s, (j,)) for j in range(2) for s in range(n - TAPER, n)]
+        units = [chunk + ((0, 1),) for chunk in chunks[: n - TAPER]]
+        units += [chunk + ((j,),) for j in range(2) for chunk in chunks[n - TAPER :]]
         n_units = len(units)
-        pe_order = [i for r in range(N_RANGES) for i in range(n_units) if chunks[units[i][0]][1] == r]
         opens = {}
         closes = {}
-        for i in pe_order:
-            r = chunks[units[i][0]][1]
-            for j in units[i][1]:
-                if (r, j) not in opens:
-                    opens[(r, j)] = i
-                closes[(r, j)] = i
+        for i in range(n_units):
+            for j in units[i][2]:
+                opens.setdefault((units[i][1], j), i)
+                closes[(units[i][1], j)] = i
         raws = {}
         grps = {}
         codes = {}
         accs = {}
         wides = {}
-        g_grps = {}
 
         def copy_on(engine, dst, src):
             if engine == "V":
@@ -94,31 +97,53 @@ def tile_naivematryoshkalinear_kernel(tc, x, W0, W1, W2, grad_out, out):
             else:
                 nc.scalar.copy(out=dst, in_=src)
 
-        def load_stack_half(gi, h, raw):
-            kind, c, r = GROUPS[gi]
-            w, row0 = weight_rows(c + h)
-            rows = w[row0 : row0 + K_PASS, RANGE * r : RANGE * r + RANGE]
-            nc.sync.dma_start(out=raw[:, h, :, :], in_=rows.rearrange("(p t) w -> p t w", t=4))
-            raws[(gi, h)] = raw[:, h, :, :]
+        holds = {"single": [], "pair": []}
+        undone = {}
 
-        def load(gi):
-            kind, c, r = GROUPS[gi]
-            if kind == "stack":
-                raw = raw_pool.tile([P, 2, 4, RANGE], BF16, name="raw", tag="raw")
-                for h in range(2):
-                    load_stack_half(gi, h, raw)
+        def load(item):
+            if item[0] == "g":
+                t = item[1]
+                raw = raw_pool.tile([P, FEATURES], BF16, name="g_raw", tag="raw")
+                nc.sync.dma_start(out=raw[:], in_=g[P * t : P * t + P, :])
+                raws[item] = raw[:]
+                return
+            c, r = item[1], item[2]
+            w, row0 = weight_rows(c)
+            if item[0] == "w":
+                raw = raw_pool.tile([P, 4, RANGE], BF16, name="w_raw", tag="raw")
+                ranges = (r,)
             else:
-                raw = raw_pool.tile([P, 4, 2 * RANGE], BF16, name="raw_pair", tag="raw")
-                w, row0 = weight_rows(c)
-                rows = w[row0 : row0 + K_PASS, RANGE * r : RANGE * r + 2 * RANGE]
-                nc.sync.dma_start(out=raw[:], in_=rows.rearrange("(p t) w -> p t w", t=4))
-                for h in range(2):
-                    raws[(gi, h)] = raw[:, :, RANGE * h : RANGE * h + RANGE]
+                raw = raw2_pool.tile([P, 4, 2 * RANGE], BF16, name="w_pair", tag="raw2")
+                ranges = (r, r + 1)
+            rows = w[row0 : row0 + K_PASS, RANGE * r : RANGE * (r + len(ranges))]
+            nc.sync.dma_start(out=raw[:], in_=rows.rearrange("(p t) w -> p t w", t=4))
+            for h in range(len(ranges)):
+                raws[("w", c, ranges[h])] = raw[:, :, RANGE * h : RANGE * h + RANGE]
 
-        def transpose_tokens(t, g_raw):
-            words = g_raw.bitcast(F32)
+        def parts(item):
+            if item[0] == "p":
+                return [("w", item[1], item[2]), ("w", item[1], item[2] + 1)]
+            return [item]
+
+        def issue_loads(loaded):
+            while loaded < len(LOADS):
+                item = LOADS[loaded]
+                kind = "pair" if item[0] == "p" else "single"
+                bufs = RAW_PAIRS if item[0] == "p" else RAW_SINGLES
+                held = holds[kind]
+                if len(held) >= bufs and any(part in undone for part in parts(held[-bufs])):
+                    break
+                held.append(item)
+                for part in parts(item):
+                    undone[part] = True
+                load(item)
+                loaded += 1
+            return loaded
+
+        def transpose_tokens(t):
+            words = raws[("g", t)].bitcast(F32)
             g_grp = grp_pool.tile([P, FEATURES], BF16, name="g_grp", tag="grp", align_bytes=64)
-            g_grps[t] = g_grp
+            grps[("g", t)] = g_grp
             grp_words = g_grp[:].bitcast(F32)
             for b in range(4):
                 xt = psum.tile([P, 4, P], F32, name="xt", tag="bank%d" % TRANSPOSE_BANKS[t][b])
@@ -131,36 +156,34 @@ def tile_naivematryoshkalinear_kernel(tc, x, W0, W1, W2, grad_out, out):
 
         def quantise_tokens(t):
             nc.vector.quantize_mx(
-                out=g_codes[:, t, :].bitcast(E5X4), scales=g_scales[:, t, :], in_=g_grps[t][:]
+                out=g_codes[:, t, :].bitcast(E5X4), scales=g_scales[:, t, :], in_=grps[("g", t)][:]
             )
 
-        def regroup(i, scalar_is_busy, in_head):
-            s, blocks = units[i]
-            raw = raws[(chunks[s][2], chunks[s][3])]
+        def regroup(i, scalar_banks, in_head):
+            c, r, blocks = units[i]
+            raw = raws[("w", c, r)]
             cols = BLOCK * len(blocks)
             base = BLOCK * blocks[0]
             if len(blocks) == 1:
-                v_cols = V_COLS_HALF
-            elif scalar_is_busy:
-                v_cols = V_COLS_BUSY
+                v_cols = min(cols, V_COLS_HALF + V_COLS_PER_BANK * scalar_banks)
             elif in_head:
                 v_cols = V_COLS_HEAD
             else:
-                v_cols = V_COLS
+                v_cols = min(cols, V_COLS + V_COLS_PER_BANK * scalar_banks)
             grp = grp_pool.tile([P, cols, 4], BF16, name="grp", tag="grp", align_bytes=64)
             nc.vector.tensor_copy(
-                out=grp[:, 0:v_cols, :].rearrange("p (c i) t -> p c t i", i=8),
-                in_=raw[:, :, base : base + v_cols].rearrange("p t (c i) -> p c t i", i=8),
+                out=grp[:, 0:v_cols, :].rearrange("p (c i) t -> p c t i", i=RUN),
+                in_=raw[:, :, base : base + v_cols].rearrange("p t (c i) -> p c t i", i=RUN),
             )
             if v_cols < cols:
                 nc.scalar.copy(
-                    out=grp[:, v_cols:cols, :].rearrange("p (c i) t -> p c t i", i=8),
-                    in_=raw[:, :, base + v_cols : base + cols].rearrange("p t (c i) -> p c t i", i=8),
+                    out=grp[:, v_cols:cols, :].rearrange("p (c i) t -> p c t i", i=RUN),
+                    in_=raw[:, :, base + v_cols : base + cols].rearrange("p t (c i) -> p c t i", i=RUN),
                 )
             grps[i] = grp
 
         def quantise(i):
-            s, blocks = units[i]
+            blocks = units[i][2]
             cols = BLOCK * len(blocks)
             cw = code_pool.tile([P, cols], U32, name="w_codes", tag="w_codes", align_bytes=64)
             cs = code_pool.tile([P, cols], U8, name="w_scales", tag="w_scales", align_bytes=64)
@@ -174,8 +197,7 @@ def tile_naivematryoshkalinear_kernel(tc, x, W0, W1, W2, grad_out, out):
                 codes[(i, blocks[k])] = (cw[:, part], cs[:, part])
 
         def multiply(i, t):
-            s, blocks = units[i]
-            c, r = chunks[s][0], chunks[s][1]
+            c, r, blocks = units[i]
             for j in blocks:
                 if opens[(r, j)] == i:
                     accs[(t, j)] = psum.tile([P, BLOCK], F32, name="acc", tag="bank%d" % (2 * t + j))
@@ -212,24 +234,16 @@ def tile_naivematryoshkalinear_kernel(tc, x, W0, W1, W2, grad_out, out):
                 copy_on("V" if j == 1 and t % 2 == 0 else "S", ost[:], accs[(t, j)][:])
                 nc.sync.dma_start(out=o[rows, col0 : col0 + BLOCK], in_=ost[:])
 
-        g_raws = []
-        for k in range(TOK_TILES // 2):
-            g_raw = raw_pool.tile([P, 2, FEATURES], BF16, name="g_raw", tag="raw")
-            w_raw = raw_pool.tile([P, 2, 4, RANGE], BF16, name="raw", tag="raw")
-            for h in range(2):
-                t = 2 * k + h
-                nc.sync.dma_start(out=g_raw[:, h, :], in_=g[P * t : P * t + P, :])
-                g_raws.append(g_raw[:, h, :])
-                load_stack_half(k, h, w_raw)
-        loaded = TOK_TILES // 2
-        for k in range(TOK_TILES, RAW_BUFS):
-            load(loaded)
-            loaded += 1
+        loaded = issue_loads(0)
 
         work = []
-        for t in range(TOK_TILES):
-            work += [("g", t), ("u", t)]
-        work += [("u", i) for i in range(TOK_TILES, n_units)]
+        for w in ORDER:
+            if w[0] == "g":
+                work.append(w)
+            elif chunks.index((w[1], w[2])) < n - TAPER:
+                work.append(("u", chunks.index((w[1], w[2]))))
+        head = max(k for k in range(len(work)) if work[k][0] == "g") + 2
+        work += [("u", i) for i in range(n - TAPER, n_units)]
         n_work = len(work)
         ready_g = {}
         ready_u = {}
@@ -244,12 +258,12 @@ def tile_naivematryoshkalinear_kernel(tc, x, W0, W1, W2, grad_out, out):
 
         pe_seq = []
         for r in range(N_RANGES):
-            products = [(i, t) for i in pe_order if chunks[units[i][0]][1] == r for t in range(TOK_TILES)]
-            pe_seq += sorted(products, key=lambda pr: (ready(pr), pe_order.index(pr[0]), pr[1]))
+            products = [(i, t) for i in range(n_units) if units[i][1] == r for t in range(TOK_TILES)]
+            start = max(ready(pr) for pr in pe_seq) + 1 if pe_seq else 0
+            early = [pr for pr in products if ready(pr) <= start]
+            late = [pr for pr in products if ready(pr) > start]
+            pe_seq += sorted(early, key=lambda pr: (pr[1], pr[0])) + sorted(late, key=lambda pr: (ready(pr), pr[0], pr[1]))
 
-        last_unit_of_group = {}
-        for i in range(n_units):
-            last_unit_of_group[chunks[units[i][0]][2]] = i
         issued = 0
         step = 0
         while issued < len(pe_seq):
@@ -257,28 +271,28 @@ def tile_naivematryoshkalinear_kernel(tc, x, W0, W1, W2, grad_out, out):
             room = PASSES_PER_STEP
             while issued + len(todo) < len(pe_seq):
                 product = pe_seq[issued + len(todo)]
-                passes = len(units[product[0]][1])
+                passes = len(units[product[0]][2])
                 if ready(product) > step or passes > room:
                     break
                 todo.append(product)
                 room -= passes
-            scalar_is_busy = False
+            scalar_banks = 0
             for i, t in todo:
-                r = chunks[units[i][0]][1]
-                if len(units[i][1]) == 2 and closes[(r, 0)] == i:
-                    scalar_is_busy = True
+                c, r, blocks = units[i]
+                for j in blocks:
+                    if closes[(r, j)] == i:
+                        scalar_banks += 1
             if step < n_work:
                 kind, a = work[step]
-                frees_a_slot = False
                 if kind == "g":
-                    transpose_tokens(a, g_raws[a])
-                    frees_a_slot = a % 2 == 1
+                    transpose_tokens(a)
+                    undone.pop(("g", a))
                 else:
-                    regroup(a, scalar_is_busy, step < 2 * TOK_TILES)
-                    frees_a_slot = last_unit_of_group[chunks[units[a][0]][2]] == a
-                if frees_a_slot and loaded < len(GROUPS):
-                    load(loaded)
-                    loaded += 1
+                    regroup(a, scalar_banks, step < head)
+                    c, r, blocks = units[a]
+                    if 1 in blocks:
+                        undone.pop(("w", c, r))
+                loaded = issue_loads(loaded)
             if 1 <= step <= n_work:
                 kind, a = work[step - 1]
                 if kind == "g":

@@ -18,7 +18,8 @@ K_PASS = 512
 N_PASS = FEATURES // K_PASS
 BLOCK = 512
 RANGE = 1024
-N_RANGES = FEATURES // RANGE
+RANGES = [3, 2, 1, 0]
+WIDE = (2, 3)
 RUN = 8
 V_COLS = 512
 V_COLS_PER_BANK = 64
@@ -26,20 +27,20 @@ V_COLS_HEAD = 704
 V_COLS_HALF = 320
 TAPER = 2
 PASSES_PER_STEP = 12
-RAW_SINGLES = 6
-RAW_PAIRS = 3
+RAW_SINGLES = 7
+RAW_PAIRS = 2
 CODE_BUFS = 6
 TRANSPOSE_BANKS = [[2, 3, 4, 5], [4, 5, 6, 7], [6, 7, 6, 7], [6, 7, 6, 7]]
 LOADS = [
-    ("g", 0), ("w", 0, 0), ("g", 1), ("w", 1, 0), ("g", 2), ("w", 4, 0), ("g", 3), ("w", 5, 0),
-    ("w", 6, 0), ("w", 7, 0), ("p", 2, 0), ("p", 3, 0), ("w", 4, 1), ("w", 5, 1), ("p", 6, 1), ("p",
-    7, 1), ("p", 4, 2), ("p", 5, 2), ("w", 6, 3), ("w", 7, 3),
+    ("g", 0), ("w", 4, 3), ("g", 1), ("w", 5, 3), ("g", 2), ("w", 6, 3), ("g", 3), ("w", 7, 3),
+    ("w", 4, 2), ("w", 5, 2), ("p", 6, 1), ("p", 7, 1), ("w", 4, 1), ("w", 5, 1), ("p", 2, 0), ("p",
+    3, 0), ("w", 0, 0), ("w", 1, 0), ("w", 4, 0), ("w", 5, 0), ("w", 6, 0), ("w", 7, 0),
 ]
 ORDER = [
-    ("g", 0), ("w", 0, 0), ("g", 1), ("w", 1, 0), ("g", 2), ("w", 4, 0), ("g", 3), ("w", 5, 0),
-    ("w", 6, 0), ("w", 7, 0), ("w", 2, 0), ("w", 2, 1), ("w", 3, 0), ("w", 3, 1), ("w", 4, 1), ("w",
-    5, 1), ("w", 6, 1), ("w", 6, 2), ("w", 7, 1), ("w", 7, 2), ("w", 4, 2), ("w", 4, 3), ("w", 5,
-    2), ("w", 5, 3), ("w", 6, 3), ("w", 7, 3),
+    ("g", 0), ("w", 4, 3), ("g", 1), ("w", 5, 3), ("g", 2), ("w", 6, 3), ("g", 3), ("w", 7, 3),
+    ("w", 4, 2), ("w", 5, 2), ("w", 6, 2), ("w", 6, 1), ("w", 7, 2), ("w", 7, 1), ("w", 4, 1), ("w",
+    5, 1), ("w", 2, 1), ("w", 3, 1), ("w", 2, 0), ("w", 3, 0), ("w", 0, 0), ("w", 1, 0), ("w", 4,
+    0), ("w", 5, 0), ("w", 6, 0), ("w", 7, 0),
 ]
 
 FLOPS = 2 * TOKENS * (1024 * 1024 + 1024 * 2048 + 2048 * 4096)
@@ -90,6 +91,7 @@ def tile_naivematryoshkalinear_kernel(tc, x, W0, W1, W2, grad_out, out):
         codes = {}
         accs = {}
         wides = {}
+        done_wide = {}
 
         def copy_on(engine, dst, src):
             if engine == "V":
@@ -214,14 +216,15 @@ def tile_naivematryoshkalinear_kernel(tc, x, W0, W1, W2, grad_out, out):
             if closes[(r, blocks[0])] != i:
                 return
             rows = slice(P * t, P * t + P)
-            if r < 2:
-                if r == 0:
+            if r in WIDE:
+                if t not in wides:
                     wides[t] = wide_pool.tile([P, 2 * RANGE], F32, name="wide", tag="wide")
                 for j in blocks:
-                    col0 = RANGE * r + BLOCK * j
+                    col0 = RANGE * (r - WIDE[0]) + BLOCK * j
                     nc.scalar.copy(out=wides[t][:, col0 : col0 + BLOCK], in_=accs[(t, j)][:])
-                if r == 1:
-                    nc.sync.dma_start(out=o[rows, 0 : 2 * RANGE], in_=wides[t][:])
+                done_wide[t] = done_wide.get(t, 0) + 1
+                if done_wide[t] == 2:
+                    nc.sync.dma_start(out=o[rows, RANGE * WIDE[0] : RANGE * WIDE[0] + 2 * RANGE], in_=wides[t][:])
             elif len(blocks) == 2:
                 ost = ost_pool.tile([P, RANGE], F32, name="ost", tag="ost")
                 for j in blocks:
@@ -257,7 +260,7 @@ def tile_naivematryoshkalinear_kernel(tc, x, W0, W1, W2, grad_out, out):
             return max(ready_u[product[0]], ready_g[product[1]])
 
         pe_seq = []
-        for r in range(N_RANGES):
+        for r in RANGES:
             products = [(i, t) for i in range(n_units) if units[i][1] == r for t in range(TOK_TILES)]
             start = max(ready(pr) for pr in pe_seq) + 1 if pe_seq else 0
             early = [pr for pr in products if ready(pr) <= start]

@@ -22,11 +22,12 @@ RANGES = [3, 2, 1, 0]
 WIDE = (2, 3)
 RUN = 8
 V_COLS = 512
-V_COLS_PER_BANK = 64
+V_COLS_PER_BANK = 48
 V_COLS_HEAD = 704
 V_COLS_HALF = 320
 TAPER = 2
 PASSES_PER_STEP = 12
+VECTOR_BANKS = ((1, 1),)
 RAW_SINGLES = 7
 RAW_PAIRS = 2
 CODE_BUFS = 6
@@ -98,6 +99,9 @@ def tile_naivematryoshkalinear_kernel(tc, x, W0, W1, W2, grad_out, out):
                 nc.vector.tensor_copy(out=dst, in_=src)
             else:
                 nc.scalar.copy(out=dst, in_=src)
+
+        def bank_engine(t, j):
+            return "V" if (t, j) in VECTOR_BANKS else "S"
 
         holds = {"single": [], "pair": []}
         undone = {}
@@ -221,14 +225,14 @@ def tile_naivematryoshkalinear_kernel(tc, x, W0, W1, W2, grad_out, out):
                     wides[t] = wide_pool.tile([P, 2 * RANGE], F32, name="wide", tag="wide")
                 for j in blocks:
                     col0 = RANGE * (r - WIDE[0]) + BLOCK * j
-                    nc.scalar.copy(out=wides[t][:, col0 : col0 + BLOCK], in_=accs[(t, j)][:])
+                    copy_on(bank_engine(t, j), wides[t][:, col0 : col0 + BLOCK], accs[(t, j)][:])
                 done_wide[t] = done_wide.get(t, 0) + 1
                 if done_wide[t] == 2:
                     nc.sync.dma_start(out=o[rows, RANGE * WIDE[0] : RANGE * WIDE[0] + 2 * RANGE], in_=wides[t][:])
             elif len(blocks) == 2:
                 ost = ost_pool.tile([P, RANGE], F32, name="ost", tag="ost")
                 for j in blocks:
-                    nc.scalar.copy(out=ost[:, BLOCK * j : BLOCK * j + BLOCK], in_=accs[(t, j)][:])
+                    copy_on(bank_engine(t, j), ost[:, BLOCK * j : BLOCK * j + BLOCK], accs[(t, j)][:])
                 nc.sync.dma_start(out=o[rows, RANGE * r : RANGE * r + RANGE], in_=ost[:])
             else:
                 j = blocks[0]
@@ -283,7 +287,7 @@ def tile_naivematryoshkalinear_kernel(tc, x, W0, W1, W2, grad_out, out):
             for i, t in todo:
                 c, r, blocks = units[i]
                 for j in blocks:
-                    if closes[(r, j)] == i:
+                    if closes[(r, j)] == i and (bank_engine(t, j) == "S" or len(blocks) == 1):
                         scalar_banks += 1
             if step < n_work:
                 kind, a = work[step]

@@ -67,7 +67,7 @@ def tile_naivematryoshkalinear_kernel(tc, x, W0, W1, W2, grad_out, out):
         grp_pool = ctx.enter_context(tc.tile_pool(name="grp", bufs=4))
         code_pool = ctx.enter_context(tc.tile_pool(name="code", bufs=CODE_BUFS))
         ost_pool = ctx.enter_context(tc.tile_pool(name="ost", bufs=6))
-        wide_pool = ctx.enter_context(tc.tile_pool(name="wide", bufs=TOK_TILES))
+        wide_pool = ctx.enter_context(tc.tile_pool(name="wide", bufs=1))
         psum = ctx.enter_context(tc.psum_pool(name="psum", bufs=1))
         ctx.enter_context(tc.manual_schedule())
 
@@ -221,19 +221,24 @@ def tile_naivematryoshkalinear_kernel(tc, x, W0, W1, W2, grad_out, out):
                 return
             rows = slice(P * t, P * t + P)
             if r in WIDE:
-                if t not in wides:
-                    wides[t] = wide_pool.tile([P, 2 * RANGE], F32, name="wide", tag="wide")
+                if "all" not in wides:
+                    wides["all"] = wide_pool.tile([P, TOK_TILES, 2 * RANGE], F32, name="wide", tag="wide")
+                wide = wides["all"]
                 for j in blocks:
                     col0 = RANGE * (r - WIDE[0]) + BLOCK * j
-                    copy_on(bank_engine(t, j), wides[t][:, col0 : col0 + BLOCK], accs[(t, j)][:])
-                done_wide[t] = done_wide.get(t, 0) + 1
-                if done_wide[t] == 2:
-                    nc.sync.dma_start(out=o[rows, RANGE * WIDE[0] : RANGE * WIDE[0] + 2 * RANGE], in_=wides[t][:])
+                    copy_on(bank_engine(t, j), wide[:, t, col0 : col0 + BLOCK], accs[(t, j)][:])
+                done_wide["all"] = done_wide.get("all", 0) + 1
+                if done_wide["all"] == 2 * TOK_TILES:
+                    cols = o[:, RANGE * WIDE[0] : RANGE * WIDE[0] + 2 * RANGE]
+                    nc.sync.dma_start(out=cols.rearrange("(t p) w -> p t w", t=TOK_TILES), in_=wide[:])
             elif len(blocks) == 2:
-                ost = ost_pool.tile([P, RANGE], F32, name="ost", tag="ost")
+                if t == 0:
+                    wides[r] = wide_pool.tile([P, TOK_TILES, RANGE], F32, name="plain", tag="plain")
                 for j in blocks:
-                    copy_on(bank_engine(t, j), ost[:, BLOCK * j : BLOCK * j + BLOCK], accs[(t, j)][:])
-                nc.sync.dma_start(out=o[rows, RANGE * r : RANGE * r + RANGE], in_=ost[:])
+                    copy_on(bank_engine(t, j), wides[r][:, t, BLOCK * j : BLOCK * j + BLOCK], accs[(t, j)][:])
+                if t == TOK_TILES - 1:
+                    cols = o[:, RANGE * r : RANGE * r + RANGE]
+                    nc.sync.dma_start(out=cols.rearrange("(t p) w -> p t w", t=TOK_TILES), in_=wides[r][:])
             else:
                 j = blocks[0]
                 col0 = RANGE * r + BLOCK * j

from contextlib import ExitStack

import concourse.mybir as mybir
from concourse.masks import make_identity

F32 = mybir.dt.float32
BF16 = mybir.dt.bfloat16
U32 = mybir.dt.uint32
U8 = mybir.dt.uint8
E4X4 = mybir.dt.float8_e4m3fn_x4
E5X4 = mybir.dt.float8_e5m2_x4

P = 128
TOKENS = 512
FEATURES = 4096
TOK_TILES = TOKENS // P
K_PASS = 512
N_PASS = FEATURES // K_PASS
BLOCK = 512
RANGE = 1024
RANGES = [3, 2, 1, 0]
WIDE = (2, 3)
RUN = 8
V_COLS = 512
V_COLS_PER_BANK = 48
V_COLS_HEAD = 704
V_COLS_HALF = 320
TAPER = 2
PASSES_PER_STEP = 12
VECTOR_BANKS = ((1, 1),)
RAW_SINGLES = 7
RAW_PAIRS = 2
CODE_BUFS = 6
TRANSPOSE_BANKS = [[2, 3, 4, 5], [4, 5, 6, 7], [6, 7, 6, 7], [6, 7, 6, 7]]
LOADS = [
    ("g", 0), ("w", 4, 3), ("g", 1), ("w", 5, 3), ("g", 2), ("w", 6, 3), ("g", 3), ("w", 7, 3),
    ("w", 4, 2), ("w", 5, 2), ("p", 6, 1), ("p", 7, 1), ("w", 4, 1), ("w", 5, 1), ("p", 2, 0), ("p",
    3, 0), ("w", 0, 0), ("w", 1, 0), ("w", 4, 0), ("w", 5, 0), ("w", 6, 0), ("w", 7, 0),
]
ORDER = [
    ("g", 0), ("w", 4, 3), ("g", 1), ("w", 5, 3), ("g", 2), ("w", 6, 3), ("g", 3), ("w", 7, 3),
    ("w", 4, 2), ("w", 5, 2), ("w", 6, 2), ("w", 6, 1), ("w", 7, 2), ("w", 7, 1), ("w", 4, 1), ("w",
    5, 1), ("w", 2, 1), ("w", 3, 1), ("w", 2, 0), ("w", 3, 0), ("w", 0, 0), ("w", 1, 0), ("w", 4,
    0), ("w", 5, 0), ("w", 6, 0), ("w", 7, 0),
]

FLOPS = 2 * TOKENS * (1024 * 1024 + 1024 * 2048 + 2048 * 4096)
BYTES = 2 * (1024 * 1024 + 1024 * 2048 + 2048 * 4096) + 2 * TOKENS * FEATURES + 4 * TOKENS * FEATURES


def tile_naivematryoshkalinear_kernel(tc, x, W0, W1, W2, grad_out, out):
    nc = tc.nc
    g = grad_out.flatten_outer_dims()
    o = out.flatten_outer_dims()

    def weight_rows(c):
        if c < 2:
            return W0, K_PASS * c
        if c < 4:
            return W1, K_PASS * (c - 2)
        return W2, K_PASS * (c - 4)

    with ExitStack() as ctx:
        const = ctx.enter_context(tc.tile_pool(name="const", bufs=1))
        raw_pool = ctx.enter_context(tc.tile_pool(name="raw", bufs=RAW_SINGLES))
        raw2_pool = ctx.enter_context(tc.tile_pool(name="raw2", bufs=RAW_PAIRS))
        grp_pool = ctx.enter_context(tc.tile_pool(name="grp", bufs=4))
        code_pool = ctx.enter_context(tc.tile_pool(name="code", bufs=CODE_BUFS))
        ost_pool = ctx.enter_context(tc.tile_pool(name="ost", bufs=6))
        wide_pool = ctx.enter_context(tc.tile_pool(name="wide", bufs=1))
        psum = ctx.enter_context(tc.psum_pool(name="psum", bufs=1))
        ctx.enter_context(tc.manual_schedule())

        ident = const.tile([P, P], F32, name="ident")
        make_identity(nc, ident[:])
        g_codes = const.tile([P, TOK_TILES, N_PASS * P], U32, name="g_codes", align_bytes=64)
        g_scales = const.tile([P, TOK_TILES, N_PASS * P], U8, name="g_scales", align_bytes=64)

        chunks = [(w[1], w[2]) for w in ORDER if w[0] == "w"]
        n = len(chunks)
        units = [chunk + ((0, 1),) for chunk in chunks[: n - TAPER]]
        units += [chunk + ((j,),) for j in range(2) for chunk in chunks[n - TAPER :]]
        n_units = len(units)
        opens = {}
        closes = {}
        for i in range(n_units):
            for j in units[i][2]:
                opens.setdefault((units[i][1], j), i)
                closes[(units[i][1], j)] = i
        raws = {}
        grps = {}
        codes = {}
        accs = {}
        wides = {}
        done_wide = {}

        def copy_on(engine, dst, src):
            if engine == "V":
                nc.vector.tensor_copy(out=dst, in_=src)
            else:
                nc.scalar.copy(out=dst, in_=src)

        def bank_engine(t, j):
            return "V" if (t, j) in VECTOR_BANKS else "S"

        holds = {"single": [], "pair": []}
        undone = {}

        def load(item):
            if item[0] == "g":
                t = item[1]
                raw = raw_pool.tile([P, FEATURES], BF16, name="g_raw", tag="raw")
                nc.sync.dma_start(out=raw[:], in_=g[P * t : P * t + P, :])
                raws[item] = raw[:]
                return
            c, r = item[1], item[2]
            w, row0 = weight_rows(c)
            if item[0] == "w":
                raw = raw_pool.tile([P, 4, RANGE], BF16, name="w_raw", tag="raw")
                ranges = (r,)
            else:
                raw = raw2_pool.tile([P, 4, 2 * RANGE], BF16, name="w_pair", tag="raw2")
                ranges = (r, r + 1)
            rows = w[row0 : row0 + K_PASS, RANGE * r : RANGE * (r + len(ranges))]
            nc.sync.dma_start(out=raw[:], in_=rows.rearrange("(p t) w -> p t w", t=4))
            for h in range(len(ranges)):
                raws[("w", c, ranges[h])] = raw[:, :, RANGE * h : RANGE * h + RANGE]

        def parts(item):
            if item[0] == "p":
                return [("w", item[1], item[2]), ("w", item[1], item[2] + 1)]
            return [item]

        def issue_loads(loaded):
            while loaded < len(LOADS):
                item = LOADS[loaded]
                kind = "pair" if item[0] == "p" else "single"
                bufs = RAW_PAIRS if item[0] == "p" else RAW_SINGLES
                held = holds[kind]
                if len(held) >= bufs and any(part in undone for part in parts(held[-bufs])):
                    break
                held.append(item)
                for part in parts(item):
                    undone[part] = True
                load(item)
                loaded += 1
            return loaded

        def transpose_tokens(t):
            words = raws[("g", t)].bitcast(F32)
            g_grp = grp_pool.tile([P, FEATURES], BF16, name="g_grp", tag="grp", align_bytes=64)
            grps[("g", t)] = g_grp
            grp_words = g_grp[:].bitcast(F32)
            for b in range(4):
                xt = psum.tile([P, 4, P], F32, name="xt", tag="bank%d" % TRANSPOSE_BANKS[t][b])
                for q in range(4):
                    c = 2 * b + q // 2
                    pass_words = words[:, 256 * c : 256 * c + 256].rearrange("r (p u) -> r u p", u=2)
                    nc.tensor.transpose(xt[:, q, :], pass_words[:, q % 2, :], ident[:])
                dst = grp_words[:, 512 * b : 512 * b + 512].rearrange("p (c r u) -> p c r u", c=2, u=2)
                nc.scalar.copy(out=dst, in_=xt[:].rearrange("p (c u) r -> p c r u", u=2))

        def quantise_tokens(t):
            nc.vector.quantize_mx(
                out=g_codes[:, t, :].bitcast(E5X4), scales=g_scales[:, t, :], in_=grps[("g", t)][:]
            )

        def regroup(i, scalar_banks, in_head):
            c, r, blocks = units[i]
            raw = raws[("w", c, r)]
            cols = BLOCK * len(blocks)
            base = BLOCK * blocks[0]
            if len(blocks) == 1:
                v_cols = min(cols, V_COLS_HALF + V_COLS_PER_BANK * scalar_banks)
            elif in_head:
                v_cols = V_COLS_HEAD
            else:
                v_cols = min(cols, V_COLS + V_COLS_PER_BANK * scalar_banks)
            grp = grp_pool.tile([P, cols, 4], BF16, name="grp", tag="grp", align_bytes=64)
            nc.vector.tensor_copy(
                out=grp[:, 0:v_cols, :].rearrange("p (c i) t -> p c t i", i=RUN),
                in_=raw[:, :, base : base + v_cols].rearrange("p t (c i) -> p c t i", i=RUN),
            )
            if v_cols < cols:
                nc.scalar.copy(
                    out=grp[:, v_cols:cols, :].rearrange("p (c i) t -> p c t i", i=RUN),
                    in_=raw[:, :, base + v_cols : base + cols].rearrange("p t (c i) -> p c t i", i=RUN),
                )
            grps[i] = grp

        def quantise(i):
            blocks = units[i][2]
            cols = BLOCK * len(blocks)
            cw = code_pool.tile([P, cols], U32, name="w_codes", tag="w_codes", align_bytes=64)
            cs = code_pool.tile([P, cols], U8, name="w_scales", tag="w_scales", align_bytes=64)
            for k in range(len(blocks)):
                part = slice(BLOCK * k, BLOCK * k + BLOCK)
                nc.vector.quantize_mx(
                    out=cw[:, part].bitcast(E4X4),
                    scales=cs[:, part],
                    in_=grps[i][:, part, :].rearrange("p w t -> p (w t)"),
                )
                codes[(i, blocks[k])] = (cw[:, part], cs[:, part])

        def multiply(i, t):
            c, r, blocks = units[i]
            for j in blocks:
                if opens[(r, j)] == i:
                    accs[(t, j)] = psum.tile([P, BLOCK], F32, name="acc", tag="bank%d" % (2 * t + j))
                cw, cs = codes[(i, j)]
                nc.tensor.matmul_mx(
                    out=accs[(t, j)][:],
                    lhsT=g_codes[:, t, P * c : P * c + P].bitcast(E5X4),
                    lhsT_scale=g_scales[:, t, P * c : P * c + P],
                    rhs=cw.bitcast(E4X4),
                    rhs_scale=cs,
                    start=opens[(r, j)] == i,
                    stop=closes[(r, j)] == i,
                )
            if closes[(r, blocks[0])] != i:
                return
            rows = slice(P * t, P * t + P)
            if r in WIDE:
                if "all" not in wides:
                    wides["all"] = wide_pool.tile([P, TOK_TILES, 2 * RANGE], F32, name="wide", tag="wide")
                wide = wides["all"]
                for j in blocks:
                    col0 = RANGE * (r - WIDE[0]) + BLOCK * j
                    copy_on(bank_engine(t, j), wide[:, t, col0 : col0 + BLOCK], accs[(t, j)][:])
                done_wide["all"] = done_wide.get("all", 0) + 1
                if done_wide["all"] == 2 * TOK_TILES:
                    cols = o[:, RANGE * WIDE[0] : RANGE * WIDE[0] + 2 * RANGE]
                    nc.sync.dma_start(out=cols.rearrange("(t p) w -> p t w", t=TOK_TILES), in_=wide[:])
            elif len(blocks) == 2:
                if t == 0:
                    wides[r] = wide_pool.tile([P, TOK_TILES, RANGE], F32, name="plain", tag="plain")
                for j in blocks:
                    copy_on(bank_engine(t, j), wides[r][:, t, BLOCK * j : BLOCK * j + BLOCK], accs[(t, j)][:])
                if t == TOK_TILES - 1:
                    cols = o[:, RANGE * r : RANGE * r + RANGE]
                    nc.sync.dma_start(out=cols.rearrange("(t p) w -> p t w", t=TOK_TILES), in_=wides[r][:])
            else:
                j = blocks[0]
                col0 = RANGE * r + BLOCK * j
                ost = ost_pool.tile([P, BLOCK], F32, name="ost_half", tag="ost")
                copy_on("V" if j == 1 and t % 2 == 0 else "S", ost[:], accs[(t, j)][:])
                nc.sync.dma_start(out=o[rows, col0 : col0 + BLOCK], in_=ost[:])

        loaded = issue_loads(0)

        work = []
        for w in ORDER:
            if w[0] == "g":
                work.append(w)
            elif chunks.index((w[1], w[2])) < n - TAPER:
                work.append(("u", chunks.index((w[1], w[2]))))
        head = max(k for k in range(len(work)) if work[k][0] == "g") + 2
        work += [("u", i) for i in range(n - TAPER, n_units)]
        n_work = len(work)
        ready_g = {}
        ready_u = {}
        for w in range(n_work):
            if work[w][0] == "g":
                ready_g[work[w][1]] = w + 2
            else:
                ready_u[work[w][1]] = w + 2

        def ready(product):
            return max(ready_u[product[0]], ready_g[product[1]])

        pe_seq = []
        for r in RANGES:
            products = [(i, t) for i in range(n_units) if units[i][1] == r for t in range(TOK_TILES)]
            start = max(ready(pr) for pr in pe_seq) + 1 if pe_seq else 0
            early = [pr for pr in products if ready(pr) <= start]
            late = [pr for pr in products if ready(pr) > start]
            pe_seq += sorted(early, key=lambda pr: (pr[1], pr[0])) + sorted(late, key=lambda pr: (ready(pr), pr[0], pr[1]))

        issued = 0
        step = 0
        while issued < len(pe_seq):
            todo = []
            room = PASSES_PER_STEP
            while issued + len(todo) < len(pe_seq):
                product = pe_seq[issued + len(todo)]
                passes = len(units[product[0]][2])
                if ready(product) > step or passes > room:
                    break
                todo.append(product)
                room -= passes
            scalar_banks = 0
            for i, t in todo:
                c, r, blocks = units[i]
                for j in blocks:
                    if closes[(r, j)] == i and (bank_engine(t, j) == "S" or len(blocks) == 1):
                        scalar_banks += 1
            if step < n_work:
                kind, a = work[step]
                if kind == "g":
                    transpose_tokens(a)
                    undone.pop(("g", a))
                else:
                    regroup(a, scalar_banks, step < head)
                    c, r, blocks = units[a]
                    if 1 in blocks:
                        undone.pop(("w", c, r))
                loaded = issue_loads(loaded)
            if 1 <= step <= n_work:
                kind, a = work[step - 1]
                if kind == "g":
                    quantise_tokens(a)
                else:
                    quantise(a)
            for i, t in todo:
                multiply(i, t)
            issued += len(todo)
            step += 1
